import numpy as np
import ml_dtypes


def mxq(x, axis, fmt="e4m3"):
    dtype, down = {"e4m3": (ml_dtypes.float8_e4m3fn, 7), "e5m2": (ml_dtypes.float8_e5m2, 14)}[fmt]
    v = np.moveaxis(np.asarray(x, np.float32).astype(ml_dtypes.bfloat16).astype(np.float64), axis, -1)
    blocks = v.reshape(v.shape[:-1] + (-1, 32))
    amax = np.abs(blocks).max(-1, keepdims=True)
    byte = np.maximum(np.where(amax > 0, np.frexp(amax)[1] - 1 + 127, 0) - down, 1)
    scale = np.exp2(byte - 127.0)
    codes = (blocks / scale).astype(np.float32).astype(dtype).astype(np.float64)
    return np.moveaxis((codes * scale).reshape(v.shape), -1, axis)


WIDE = False


def mx_kscale(k):
    if not WIDE:
        return np.ones(k)
    levels = np.array([10, -10, 5, -5, 0])
    a = np.random.permutation(np.resize(levels, k // 512 * 4)).reshape(k // 512, 4)
    idx = np.arange(k)
    return np.exp2(a[idx // 512, idx % 128 // 32])


BF16 = ml_dtypes.bfloat16


def bf(x):
    return np.asarray(x, np.float32).astype(BF16)


def f64(x):
    return np.asarray(x).astype(np.float64)


N, C, HH, WW = 4, 1024, 16, 16
S = HH * WW
EPS = 1e-5


def setup_inputs():
    s = mx_kscale(C)
    contrast = np.exp2(np.random.uniform(-8.0, 1.0, (N, 1, HH, WW)))
    shift = 0.5 * np.random.standard_normal((N, 1, HH, WW))
    w = 1.0 / np.sqrt(C)
    return {"x": bf(contrast * (np.random.standard_normal((N, C, HH, WW)) + shift)),
            "ln_gamma": bf((1.0 + 0.1 * np.random.standard_normal(C)) * s),
            "ln_beta": bf(0.3 * np.random.standard_normal(C) * s),
            "Wq": bf(np.random.standard_normal((C, C)) * w / s[None, :]),
            "bq": bf(0.3 * np.random.standard_normal(C)),
            "Wk": bf(np.random.standard_normal((C, C)) * w / s[None, :]),
            "bk": bf(0.3 * np.random.standard_normal(C)),
            "Wv": bf(np.random.standard_normal((C, C)) * w / s[None, :]),
            "bv": bf(0.3 * np.random.standard_normal(C))}


def reference(x, ln_gamma, ln_beta, Wq, bq, Wk, bk, Wv, bv):
    xs = f64(x).reshape(N, C, S).swapaxes(1, 2)
    mu = xs.mean(-1, keepdims=True)
    var = xs.var(-1, keepdims=True)
    x_ln = (xs - mu) / np.sqrt(var + EPS) * f64(ln_gamma) + f64(ln_beta)
    xq = mxq(x_ln, 2, "e4m3")
    q = (xq @ mxq(f64(Wq), 1, "e4m3").T) + f64(bq)
    k = (xq @ mxq(f64(Wk), 1, "e4m3").T) + f64(bk)
    v = (xq @ mxq(f64(Wv), 1, "e4m3").T) + f64(bv)
    return q, k, v

@@ -1,0 +1,238 @@
+from contextlib import ExitStack
+
+import concourse.mybir as mybir
+from concourse.masks import make_identity
+
+BF16 = mybir.dt.bfloat16
+F32 = mybir.dt.float32
+U32 = mybir.dt.uint32
+U8 = mybir.dt.uint8
+FP8X4 = mybir.dt.float8_e4m3fn_x4
+ACT = mybir.ActivationFunctionType
+ALU = mybir.AluOpType
+
+P = 128
+IMAGES = 4
+CHANNELS = 1024
+IMAGE_PIXELS = 256
+OUTPUTS = 1024
+PROJECTIONS = 3
+EPS = 1e-5
+
+PACK = 4
+PASSES = CHANNELS // (P * PACK)
+CHUNKS = CHANNELS // P
+STRIPS = IMAGE_PIXELS // P
+BANK = 512
+OUTPUT_GROUPS = OUTPUTS // BANK
+STATS_WIDTH = 512
+STATS_CALLS = CHANNELS // STATS_WIDTH
+STATS_DIM = 6
+
+FLOPS = 2 * IMAGES * IMAGE_PIXELS * CHANNELS * PROJECTIONS * OUTPUTS
+
+
+def tile_selfscaleddotproductattention2d_pa_kernel(
+    tc, x, ln_gamma, ln_beta, Wq, bq, Wk, bk, Wv, bv, out_0, out_1, out_2
+):
+    nc = tc.nc
+    weights = (Wq, Wk, Wv)
+    biases = (bq, bk, bv)
+    outs = (out_0, out_1, out_2)
+
+    with ExitStack() as ctx:
+        keep = ctx.enter_context(tc.tile_pool(name="keep", bufs=1))
+        per_weight = ctx.enter_context(tc.tile_pool(name="per_weight", bufs=PROJECTIONS))
+        work = ctx.enter_context(tc.tile_pool(name="work", bufs=2))
+        psum_t = ctx.enter_context(tc.psum_pool(name="psum_t", bufs=4))
+        psum_acc = ctx.enter_context(tc.psum_pool(name="psum_acc", bufs=4))
+
+        ident_bf = keep.tile([P, P], BF16)
+        make_identity(nc, ident_bf[:])
+        ident_f = keep.tile([P, P], F32)
+        make_identity(nc, ident_f[:])
+
+        x_sb = keep.tile([P, IMAGES, CHUNKS // 2, 2 * IMAGE_PIXELS], BF16)
+        for n in range(IMAGES):
+            nc.sync.dma_start(
+                out=x_sb[:, n], in_=x[n].rearrange("(a p e) h w -> p a (e h w)", p=P, e=2)
+            )
+
+        gamma_bf = keep.tile([P, CHUNKS], BF16)
+        beta_bf = keep.tile([P, CHUNKS], BF16)
+        for vector_sb, vector in ((gamma_bf, ln_gamma), (beta_bf, ln_beta)):
+            nc.scalar.dma_start(
+                out=vector_sb[:].rearrange("p (a e) -> p a e", e=2),
+                in_=vector.rearrange("(a p e) -> p a e", p=P, e=2),
+            )
+        gamma = keep.tile([P, CHUNKS], F32)
+        beta = keep.tile([P, CHUNKS], F32)
+        nc.vector.tensor_copy(out=gamma[:], in_=gamma_bf[:])
+        nc.vector.tensor_copy(out=beta[:], in_=beta_bf[:])
+
+        w_sbs = []
+        bias_sb = keep.tile([P, PROJECTIONS, OUTPUTS], BF16)
+        for i in range(PROJECTIONS):
+            w_sb = per_weight.tile([P, OUTPUTS // P, CHANNELS], BF16, name="w_sb")
+            rows = weights[i].rearrange("(r p) k -> p r k", p=P)
+            for oc in range(OUTPUT_GROUPS):
+                r_range = slice(oc * (BANK // P), (oc + 1) * (BANK // P))
+                nc.sync.dma_start(out=w_sb[:, r_range, :], in_=rows[:, r_range, :])
+            nc.sync.dma_start(out=bias_sb[:, i, :], in_=biases[i].partition_broadcast(P))
+            w_sbs.append(w_sb)
+
+        mean_var = keep.tile([P, IMAGES * STRIPS, 2], F32)
+        var_eps = keep.tile([P, IMAGES * STRIPS], F32)
+        std = keep.tile([P, IMAGES * STRIPS], F32)
+        rstd = keep.tile([P, IMAGES * STRIPS], F32)
+        shift = keep.tile([P, IMAGES * STRIPS], F32)
+        x_ln = keep.tile([P, CHUNKS, IMAGES * IMAGE_PIXELS], BF16)
+        x_codes = keep.tile([P, IMAGES, PASSES, IMAGE_PIXELS], U32, align_bytes=64)
+        x_scales = keep.tile([P, IMAGES, PASSES, IMAGE_PIXELS], U8, align_bytes=64)
+        w_codes = []
+        w_scales = []
+        for i in range(PROJECTIONS):
+            w_codes.append(
+                per_weight.tile([P, OUTPUT_GROUPS, PASSES, BANK], U32, align_bytes=64, name="w_codes")
+            )
+            w_scales.append(
+                per_weight.tile([P, OUTPUT_GROUPS, PASSES, BANK], U8, align_bytes=64, name="w_scales")
+            )
+
+        def normalise_image(n):
+            strips = slice(n * STRIPS, (n + 1) * STRIPS)
+            image_pixels = slice(n * IMAGE_PIXELS, (n + 1) * IMAGE_PIXELS)
+            transposed = []
+            for h in range(STRIPS):
+                x_t = psum_t.tile([P, CHANNELS], BF16, tag="t", name="x_t")
+                for m in range(CHUNKS):
+                    a, e = divmod(m, 2)
+                    first = e * IMAGE_PIXELS + h * P
+                    nc.tensor.transpose(
+                        out=x_t[:, m * P : (m + 1) * P],
+                        in_=x_sb[:, n, a, first : first + P],
+                        identity=ident_bf[:],
+                    )
+                stats = work.tile([P, STATS_CALLS, STATS_DIM], F32)
+                for s in range(STATS_CALLS):
+                    nc.vector.bn_stats(
+                        out=stats[:, s, :], in_=x_t[:, s * STATS_WIDTH : (s + 1) * STATS_WIDTH]
+                    )
+                nc.vector.bn_aggr(
+                    out=mean_var[:, n * STRIPS + h, :], in_=stats[:].rearrange("p s d -> p (s d)")
+                )
+                transposed.append(x_t)
+
+            nc.vector.tensor_scalar_add(out=var_eps[:, strips], in0=mean_var[:, strips, 1], scalar1=EPS)
+            nc.scalar.activation(out=std[:, strips], in_=var_eps[:, strips], func=ACT.Sqrt)
+            nc.vector.reciprocal(out=rstd[:, strips], in_=std[:, strips])
+            nc.vector.scalar_tensor_tensor(
+                out=shift[:, strips],
+                in0=mean_var[:, strips, 0],
+                scalar=-1.0,
+                in1=rstd[:, strips],
+                op0=ALU.mult,
+                op1=ALU.mult,
+            )
+
+            normed = []
+            for h in range(STRIPS):
+                b = n * STRIPS + h
+                z = work.tile([P, CHANNELS], F32, name="z", bufs=2 * STRIPS)
+                nc.scalar.activation(
+                    out=z[:],
+                    in_=transposed[h][:],
+                    func=ACT.Identity,
+                    bias=shift[:, b : b + 1],
+                    scale=rstd[:, b : b + 1],
+                )
+                normed.append(z)
+
+            for first_chunk in range(0, CHUNKS, 2):
+                z_t = psum_t.tile([P, 2, IMAGE_PIXELS], F32, tag="t", name="z_t")
+                for c in range(2):
+                    m = first_chunk + c
+                    for h in range(STRIPS):
+                        nc.tensor.transpose(
+                            out=z_t[:, c, h * P : (h + 1) * P],
+                            in_=normed[h][:, m * P : (m + 1) * P],
+                            identity=ident_f[:],
+                        )
+                for c in range(2):
+                    m = first_chunk + c
+                    nc.scalar.activation(
+                        out=x_ln[:, m, image_pixels],
+                        in_=z_t[:, c, :],
+                        func=ACT.Identity,
+                        bias=beta[:, m : m + 1],
+                        scale=gamma[:, m : m + 1],
+                    )
+
+            x_grouped = work.tile([P, PASSES, IMAGE_PIXELS, PACK], BF16, align_bytes=64)
+            nc.vector.tensor_copy(
+                out=x_grouped[:],
+                in_=x_ln[:, :, image_pixels].rearrange("p (g t) s -> p g s t", t=PACK),
+            )
+            nc.vector.quantize_mx(
+                out=x_codes[:, n].rearrange("p g s -> p (g s)").bitcast(FP8X4),
+                scales=x_scales[:, n].rearrange("p g s -> p (g s)"),
+                in_=x_grouped[:].rearrange("p g s t -> p (g s t)"),
+            )
+
+        def prepare_weight(i):
+            for oc in range(OUTPUT_GROUPS):
+                w_grouped = work.tile([P, PASSES * BANK * PACK], BF16, align_bytes=64, bufs=3)
+                w_grouped_words = w_grouped[:].bitcast(F32)
+                for g in range(PASSES):
+                    for pair in range(BANK // (2 * P)):
+                        w_t = psum_t.tile([P, 2, 2 * P], F32, tag="t", name="w_t")
+                        for u in range(2):
+                            for rr in range(2):
+                                r = oc * (BANK // P) + 2 * pair + rr
+                                first = (2 * g + u) * P
+                                nc.tensor.transpose(
+                                    out=w_t[:, u, rr * P : (rr + 1) * P],
+                                    in_=w_sbs[i][:, r, :].bitcast(F32)[:, first : first + P],
+                                    identity=ident_f[:],
+                                )
+                        first_word = (g * BANK + pair * 2 * P) * 2
+                        nc.scalar.copy(
+                            out=w_grouped_words[:, first_word : first_word + BANK].rearrange(
+                                "p (o u) -> p o u", u=2
+                            ),
+                            in_=w_t[:].rearrange("p u o -> p o u"),
+                        )
+                nc.vector.quantize_mx(
+                    out=w_codes[i][:, oc].rearrange("p g o -> p (g o)").bitcast(FP8X4),
+                    scales=w_scales[i][:, oc].rearrange("p g o -> p (g o)"),
+                    in_=w_grouped[:],
+                )
+
+        def project(n, i):
+            for h in range(STRIPS):
+                strip = slice(h * P, (h + 1) * P)
+                result = work.tile([P, OUTPUTS], F32, bufs=4)
+                for oc in range(OUTPUT_GROUPS):
+                    acc = psum_acc.tile([P, BANK], F32)
+                    for g in range(PASSES):
+                        nc.tensor.matmul_mx(
+                            out=acc[:],
+                            lhsT=x_codes[:, n, g, strip].bitcast(FP8X4),
+                            lhsT_scale=x_scales[:, n, g, strip],
+                            rhs=w_codes[i][:, oc, g, :].bitcast(FP8X4),
+                            rhs_scale=w_scales[i][:, oc, g, :],
+                            start=(g == 0),
+                            stop=(g == PASSES - 1),
+                        )
+                    out_cols = slice(oc * BANK, (oc + 1) * BANK)
+                    nc.vector.tensor_tensor(
+                        out=result[:, out_cols], in0=acc[:], in1=bias_sb[:, i, out_cols], op=ALU.add
+                    )
+                nc.sync.dma_start(out=outs[i][n, strip, :], in_=result[:])
+
+        for n in range(IMAGES):
+            normalise_image(n)
+            for i in range(PROJECTIONS):
+                if n == 0:
+                    prepare_weight(i)
+                project(n, i)

@@ -24,7 +24,8 @@ PASSES = CHANNELS // (P * PACK)
 CHUNKS = CHANNELS // P
 STRIPS = IMAGE_PIXELS // P
 BANK = 512
-OUTPUT_GROUPS = OUTPUTS // BANK
+HALVES = OUTPUTS // BANK
+UNIT_BANKS = 4
 STATS_WIDTH = 512
 STATS_CALLS = CHANNELS // STATS_WIDTH
 STATS_DIM = 6
@@ -44,13 +45,9 @@ def tile_selfscaleddotproductattention2d_pa_kernel(
         keep = ctx.enter_context(tc.tile_pool(name="keep", bufs=1))
         per_weight = ctx.enter_context(tc.tile_pool(name="per_weight", bufs=PROJECTIONS))
         work = ctx.enter_context(tc.tile_pool(name="work", bufs=2))
-        psum_t = ctx.enter_context(tc.psum_pool(name="psum_t", bufs=4))
+        psum_unit = ctx.enter_context(tc.psum_pool(name="psum_unit", bufs=UNIT_BANKS))
         psum_acc = ctx.enter_context(tc.psum_pool(name="psum_acc", bufs=4))
-
-        ident_bf = keep.tile([P, P], BF16)
-        make_identity(nc, ident_bf[:])
-        ident_f = keep.tile([P, P], F32)
-        make_identity(nc, ident_f[:])
+        ctx.enter_context(tc.manual_schedule())
 
         x_sb = keep.tile([P, IMAGES, CHUNKS // 2, 2 * IMAGE_PIXELS], BF16)
         for n in range(IMAGES):
@@ -65,46 +62,47 @@ def tile_selfscaleddotproductattention2d_pa_kernel(
                 out=vector_sb[:].rearrange("p (a e) -> p a e", e=2),
                 in_=vector.rearrange("(a p e) -> p a e", p=P, e=2),
             )
-        gamma = keep.tile([P, CHUNKS], F32)
-        beta = keep.tile([P, CHUNKS], F32)
-        nc.vector.tensor_copy(out=gamma[:], in_=gamma_bf[:])
-        nc.vector.tensor_copy(out=beta[:], in_=beta_bf[:])
 
         w_sbs = []
         bias_sb = keep.tile([P, PROJECTIONS, OUTPUTS], BF16)
         for i in range(PROJECTIONS):
             w_sb = per_weight.tile([P, OUTPUTS // P, CHANNELS], BF16, name="w_sb")
             rows = weights[i].rearrange("(r p) k -> p r k", p=P)
-            for oc in range(OUTPUT_GROUPS):
+            for oc in range(HALVES):
                 r_range = slice(oc * (BANK // P), (oc + 1) * (BANK // P))
                 nc.sync.dma_start(out=w_sb[:, r_range, :], in_=rows[:, r_range, :])
             nc.sync.dma_start(out=bias_sb[:, i, :], in_=biases[i].partition_broadcast(P))
             w_sbs.append(w_sb)
 
+        ident_bf = keep.tile([P, P], BF16)
+        make_identity(nc, ident_bf[:])
+        ident_f = keep.tile([P, P], F32)
+        make_identity(nc, ident_f[:])
+        minus_half = keep.tile([P, STRIPS], F32)
+        nc.gpsimd.memset(minus_half[:], -0.5)
+        gamma = keep.tile([P, CHUNKS], F32)
+        beta = keep.tile([P, CHUNKS], F32)
+        nc.gpsimd.tensor_copy(out=gamma[:], in_=gamma_bf[:])
+        nc.gpsimd.tensor_copy(out=beta[:], in_=beta_bf[:])
+
+        x_pix = keep.tile([P, IMAGES * STRIPS, CHANNELS], BF16)
         mean_var = keep.tile([P, IMAGES * STRIPS, 2], F32)
         var_eps = keep.tile([P, IMAGES * STRIPS], F32)
-        std = keep.tile([P, IMAGES * STRIPS], F32)
         rstd = keep.tile([P, IMAGES * STRIPS], F32)
-        shift = keep.tile([P, IMAGES * STRIPS], F32)
-        x_ln = keep.tile([P, CHUNKS, IMAGES * IMAGE_PIXELS], BF16)
+        minus_mean = keep.tile([P, IMAGES * STRIPS], F32)
         x_codes = keep.tile([P, IMAGES, PASSES, IMAGE_PIXELS], U32, align_bytes=64)
         x_scales = keep.tile([P, IMAGES, PASSES, IMAGE_PIXELS], U8, align_bytes=64)
         w_codes = []
         w_scales = []
         for i in range(PROJECTIONS):
-            w_codes.append(
-                per_weight.tile([P, OUTPUT_GROUPS, PASSES, BANK], U32, align_bytes=64, name="w_codes")
-            )
-            w_scales.append(
-                per_weight.tile([P, OUTPUT_GROUPS, PASSES, BANK], U8, align_bytes=64, name="w_scales")
-            )
+            w_codes.append(per_weight.tile([P, HALVES, PASSES, BANK], U32, align_bytes=64, name="w_codes"))
+            w_scales.append(per_weight.tile([P, HALVES, PASSES, BANK], U8, align_bytes=64, name="w_scales"))
+        normed = []
 
         def normalise_image(n):
             strips = slice(n * STRIPS, (n + 1) * STRIPS)
-            image_pixels = slice(n * IMAGE_PIXELS, (n + 1) * IMAGE_PIXELS)
-            transposed = []
             for h in range(STRIPS):
-                x_t = psum_t.tile([P, CHANNELS], BF16, tag="t", name="x_t")
+                x_t = psum_unit.tile([P, CHANNELS], BF16, tag="unit", name="x_t")
                 for m in range(CHUNKS):
                     a, e = divmod(m, 2)
                     first = e * IMAGE_PIXELS + h * P
@@ -113,126 +111,158 @@ def tile_selfscaleddotproductattention2d_pa_kernel(
                         in_=x_sb[:, n, a, first : first + P],
                         identity=ident_bf[:],
                     )
+                nc.scalar.copy(out=x_pix[:, n * STRIPS + h, :], in_=x_t[:])
+            for h in range(STRIPS):
+                b = n * STRIPS + h
                 stats = work.tile([P, STATS_CALLS, STATS_DIM], F32)
                 for s in range(STATS_CALLS):
                     nc.vector.bn_stats(
-                        out=stats[:, s, :], in_=x_t[:, s * STATS_WIDTH : (s + 1) * STATS_WIDTH]
+                        out=stats[:, s, :], in_=x_pix[:, b, s * STATS_WIDTH : (s + 1) * STATS_WIDTH]
                     )
-                nc.vector.bn_aggr(
-                    out=mean_var[:, n * STRIPS + h, :], in_=stats[:].rearrange("p s d -> p (s d)")
-                )
-                transposed.append(x_t)
-
-            nc.vector.tensor_scalar_add(out=var_eps[:, strips], in0=mean_var[:, strips, 1], scalar1=EPS)
-            nc.scalar.activation(out=std[:, strips], in_=var_eps[:, strips], func=ACT.Sqrt)
-            nc.vector.reciprocal(out=rstd[:, strips], in_=std[:, strips])
-            nc.vector.scalar_tensor_tensor(
-                out=shift[:, strips],
-                in0=mean_var[:, strips, 0],
-                scalar=-1.0,
-                in1=rstd[:, strips],
-                op0=ALU.mult,
-                op1=ALU.mult,
+                nc.vector.bn_aggr(out=mean_var[:, b, :], in_=stats[:].rearrange("p s d -> p (s d)"))
+            nc.gpsimd.tensor_scalar(
+                out=var_eps[:, strips], in0=mean_var[:, strips, 1], scalar1=EPS, scalar2=1.0,
+                op0=ALU.add, op1=ALU.mult,
             )
-
-            normed = []
+            nc.gpsimd.tensor_tensor(out=rstd[:, strips], in0=var_eps[:, strips], in1=minus_half[:], op=ALU.pow)
+            nc.gpsimd.tensor_scalar(
+                out=minus_mean[:, strips], in0=mean_var[:, strips, 0], scalar1=-1.0, scalar2=0.0,
+                op0=ALU.mult, op1=ALU.add,
+            )
             for h in range(STRIPS):
                 b = n * STRIPS + h
-                z = work.tile([P, CHANNELS], F32, name="z", bufs=2 * STRIPS)
-                nc.scalar.activation(
-                    out=z[:],
-                    in_=transposed[h][:],
-                    func=ACT.Identity,
-                    bias=shift[:, b : b + 1],
-                    scale=rstd[:, b : b + 1],
+                z = keep.tile([P, CHANNELS], F32, name="z%d" % b)
+                nc.gpsimd.tensor_scalar(
+                    out=z[:], in0=x_pix[:, b, :], scalar1=minus_mean[:, b : b + 1], scalar2=rstd[:, b : b + 1],
+                    op0=ALU.add, op1=ALU.mult,
                 )
                 normed.append(z)
 
+        def image_transposes(n):
+            banks = []
             for first_chunk in range(0, CHUNKS, 2):
-                z_t = psum_t.tile([P, 2, IMAGE_PIXELS], F32, tag="t", name="z_t")
+                z_t = psum_unit.tile([P, 2, IMAGE_PIXELS], F32, tag="unit", name="z_t")
                 for c in range(2):
                     m = first_chunk + c
                     for h in range(STRIPS):
                         nc.tensor.transpose(
                             out=z_t[:, c, h * P : (h + 1) * P],
-                            in_=normed[h][:, m * P : (m + 1) * P],
+                            in_=normed[n * STRIPS + h][:, m * P : (m + 1) * P],
                             identity=ident_f[:],
                         )
-                for c in range(2):
-                    m = first_chunk + c
-                    nc.scalar.activation(
-                        out=x_ln[:, m, image_pixels],
-                        in_=z_t[:, c, :],
-                        func=ACT.Identity,
-                        bias=beta[:, m : m + 1],
-                        scale=gamma[:, m : m + 1],
-                    )
+                banks.append(z_t)
+            return banks
 
+        def image_gain_and_shift(banks):
+            x_ln = work.tile([P, CHUNKS, IMAGE_PIXELS], BF16)
+            for m in range(CHUNKS):
+                nc.scalar.activation(
+                    out=x_ln[:, m, :],
+                    in_=banks[m // 2][:, m % 2, :],
+                    func=ACT.Identity,
+                    bias=beta[:, m : m + 1],
+                    scale=gamma[:, m : m + 1],
+                )
+            return x_ln
+
+        def image_quantise(n, x_ln):
             x_grouped = work.tile([P, PASSES, IMAGE_PIXELS, PACK], BF16, align_bytes=64)
-            nc.vector.tensor_copy(
-                out=x_grouped[:],
-                in_=x_ln[:, :, image_pixels].rearrange("p (g t) s -> p g s t", t=PACK),
-            )
+            nc.vector.tensor_copy(out=x_grouped[:], in_=x_ln[:].rearrange("p (g t) s -> p g s t", t=PACK))
             nc.vector.quantize_mx(
                 out=x_codes[:, n].rearrange("p g s -> p (g s)").bitcast(FP8X4),
                 scales=x_scales[:, n].rearrange("p g s -> p (g s)"),
                 in_=x_grouped[:].rearrange("p g s t -> p (g s t)"),
             )
 
-        def prepare_weight(i):
-            for oc in range(OUTPUT_GROUPS):
-                w_grouped = work.tile([P, PASSES * BANK * PACK], BF16, align_bytes=64, bufs=3)
-                w_grouped_words = w_grouped[:].bitcast(F32)
-                for g in range(PASSES):
-                    for pair in range(BANK // (2 * P)):
-                        w_t = psum_t.tile([P, 2, 2 * P], F32, tag="t", name="w_t")
-                        for u in range(2):
-                            for rr in range(2):
-                                r = oc * (BANK // P) + 2 * pair + rr
-                                first = (2 * g + u) * P
-                                nc.tensor.transpose(
-                                    out=w_t[:, u, rr * P : (rr + 1) * P],
-                                    in_=w_sbs[i][:, r, :].bitcast(F32)[:, first : first + P],
-                                    identity=ident_f[:],
-                                )
-                        first_word = (g * BANK + pair * 2 * P) * 2
-                        nc.scalar.copy(
-                            out=w_grouped_words[:, first_word : first_word + BANK].rearrange(
-                                "p (o u) -> p o u", u=2
-                            ),
-                            in_=w_t[:].rearrange("p u o -> p o u"),
-                        )
-                nc.vector.quantize_mx(
-                    out=w_codes[i][:, oc].rearrange("p g o -> p (g o)").bitcast(FP8X4),
-                    scales=w_scales[i][:, oc].rearrange("p g o -> p (g o)"),
-                    in_=w_grouped[:],
-                )
+        def weight_transposes(i, oc):
+            banks = []
+            for g in range(PASSES):
+                for pair in range(BANK // (2 * P)):
+                    w_t = psum_unit.tile([P, 2, 2 * P], F32, tag="unit", name="w_t")
+                    for u in range(2):
+                        for rr in range(2):
+                            r = oc * (BANK // P) + 2 * pair + rr
+                            first = (2 * g + u) * P
+                            nc.tensor.transpose(
+                                out=w_t[:, u, rr * P : (rr + 1) * P],
+                                in_=w_sbs[i][:, r, :].bitcast(F32)[:, first : first + P],
+                                identity=ident_f[:],
+                            )
+                    banks.append(w_t)
+            return banks
 
-        def project(n, i):
-            for h in range(STRIPS):
-                strip = slice(h * P, (h + 1) * P)
-                result = work.tile([P, OUTPUTS], F32, bufs=4)
-                for oc in range(OUTPUT_GROUPS):
-                    acc = psum_acc.tile([P, BANK], F32)
-                    for g in range(PASSES):
-                        nc.tensor.matmul_mx(
-                            out=acc[:],
-                            lhsT=x_codes[:, n, g, strip].bitcast(FP8X4),
-                            lhsT_scale=x_scales[:, n, g, strip],
-                            rhs=w_codes[i][:, oc, g, :].bitcast(FP8X4),
-                            rhs_scale=w_scales[i][:, oc, g, :],
-                            start=(g == 0),
-                            stop=(g == PASSES - 1),
-                        )
-                    out_cols = slice(oc * BANK, (oc + 1) * BANK)
-                    nc.vector.tensor_tensor(
-                        out=result[:, out_cols], in0=acc[:], in1=bias_sb[:, i, out_cols], op=ALU.add
+        def weight_copies(banks):
+            w_grouped = work.tile([P, PASSES * BANK * PACK], BF16, align_bytes=64)
+            w_grouped_words = w_grouped[:].bitcast(F32)
+            for k in range(UNIT_BANKS):
+                nc.scalar.copy(
+                    out=w_grouped_words[:, k * BANK : (k + 1) * BANK].rearrange("p (o u) -> p o u", u=2),
+                    in_=banks[k][:].rearrange("p u o -> p o u"),
+                )
+            return w_grouped
+
+        def weight_quantise(i, oc, w_grouped):
+            nc.vector.quantize_mx(
+                out=w_codes[i][:, oc].rearrange("p g o -> p (g o)").bitcast(FP8X4),
+                scales=w_scales[i][:, oc].rearrange("p g o -> p (g o)"),
+                in_=w_grouped[:],
+            )
+
+        def project(strip_index):
+            n, rest = divmod(strip_index, PROJECTIONS * STRIPS)
+            i, h = divmod(rest, STRIPS)
+            strip = slice(h * P, (h + 1) * P)
+            result = work.tile([P, OUTPUTS], F32, bufs=4)
+            for oc in range(HALVES):
+                acc = psum_acc.tile([P, BANK], F32)
+                for g in range(PASSES):
+                    nc.tensor.matmul_mx(
+                        out=acc[:],
+                        lhsT=x_codes[:, n, g, strip].bitcast(FP8X4),
+                        lhsT_scale=x_scales[:, n, g, strip],
+                        rhs=w_codes[i][:, oc, g, :].bitcast(FP8X4),
+                        rhs_scale=w_scales[i][:, oc, g, :],
+                        start=(g == 0),
+                        stop=(g == PASSES - 1),
                     )
-                nc.sync.dma_start(out=outs[i][n, strip, :], in_=result[:])
+                out_cols = slice(oc * BANK, (oc + 1) * BANK)
+                nc.vector.tensor_tensor(
+                    out=result[:, out_cols], in0=acc[:], in1=bias_sb[:, i, out_cols], op=ALU.add
+                )
+            nc.sync.dma_start(out=outs[i][n, strip, :], in_=result[:])
 
         for n in range(IMAGES):
             normalise_image(n)
-            for i in range(PROJECTIONS):
-                if n == 0:
-                    prepare_weight(i)
-                project(n, i)
+
+        banks = weight_transposes(0, 0)
+        w_grouped = weight_copies(banks)
+        banks = image_transposes(0)
+        weight_quantise(0, 0, w_grouped)
+
+        x_ln = image_gain_and_shift(banks)
+        banks = weight_transposes(0, 1)
+        image_quantise(0, x_ln)
+
+        projected = 0
+        weight_halves = PROJECTIONS * HALVES
+        for half_index in range(1, weight_halves):
+            i, oc = divmod(half_index, HALVES)
+            w_grouped = weight_copies(banks)
+            if half_index + 1 < weight_halves:
+                banks = weight_transposes((half_index + 1) // HALVES, (half_index + 1) % HALVES)
+            else:
+                banks = image_transposes(1)
+            weight_quantise(i, oc, w_grouped)
+            project(projected)
+            projected += 1
+
+        for n in range(1, IMAGES):
+            x_ln = image_gain_and_shift(banks)
+            if n + 1 < IMAGES:
+                banks = image_transposes(n + 1)
+            image_quantise(n, x_ln)
+            project(projected)
+            projected += 1
+
+        for strip_index in range(projected, IMAGES * PROJECTIONS * STRIPS):
+            project(strip_index)

@@ -106,10 +106,12 @@ def tile_selfscaleddotproductattention2d_pa_kernel(
                 for m in range(CHUNKS):
                     a, e = divmod(m, 2)
                     first = e * IMAGE_PIXELS + h * P
-                    nc.tensor.transpose(
+                    nc.tensor.matmul(
                         out=x_t[:, m * P : (m + 1) * P],
-                        in_=x_sb[:, n, a, first : first + P],
-                        identity=ident_bf[:],
+                        lhsT=x_sb[:, n, a, first : first + P],
+                        rhs=ident_bf[:],
+                        start=True,
+                        stop=True,
                     )
                 nc.scalar.copy(out=x_pix[:, n * STRIPS + h, :], in_=x_t[:])
             for h in range(STRIPS):

@@ -26,6 +26,10 @@ STRIPS = IMAGE_PIXELS // P
 BANK = 512
 HALVES = OUTPUTS // BANK
 UNIT_BANKS = 4
+RUN = 4
+SHARE = 3
+FIRST_LATE_IMAGE = 2
+LEAD = 2
 STATS_WIDTH = 512
 STATS_CALLS = CHANNELS // STATS_WIDTH
 STATS_DIM = 6
@@ -106,12 +110,10 @@ def tile_selfscaleddotproductattention2d_pa_kernel(
                 for m in range(CHUNKS):
                     a, e = divmod(m, 2)
                     first = e * IMAGE_PIXELS + h * P
-                    nc.tensor.matmul(
+                    nc.tensor.transpose(
                         out=x_t[:, m * P : (m + 1) * P],
-                        lhsT=x_sb[:, n, a, first : first + P],
-                        rhs=ident_bf[:],
-                        start=True,
-                        stop=True,
+                        in_=x_sb[:, n, a, first : first + P],
+                        identity=ident_bf[:],
                     )
                 nc.scalar.copy(out=x_pix[:, n * STRIPS + h, :], in_=x_t[:])
             for h in range(STRIPS):
@@ -169,7 +171,11 @@ def tile_selfscaleddotproductattention2d_pa_kernel(
 
         def image_quantise(n, x_ln):
             x_grouped = work.tile([P, PASSES, IMAGE_PIXELS, PACK], BF16, align_bytes=64)
-            nc.vector.tensor_copy(out=x_grouped[:], in_=x_ln[:].rearrange("p (g t) s -> p g s t", t=PACK))
+            for g in range(PASSES):
+                nc.vector.tensor_copy(
+                    out=x_grouped[:, g].rearrange("p (c i) t -> p c t i", i=RUN),
+                    in_=x_ln[:, g * PACK : (g + 1) * PACK, :].rearrange("p t (c i) -> p c t i", i=RUN),
+                )
             nc.vector.quantize_mx(
                 out=x_codes[:, n].rearrange("p g s -> p (g s)").bitcast(FP8X4),
                 scales=x_scales[:, n].rearrange("p g s -> p (g s)"),
@@ -210,7 +216,7 @@ def tile_selfscaleddotproductattention2d_pa_kernel(
                 in_=w_grouped[:],
             )
 
-        def project(strip_index):
+        def project(strip_index, helped):
             n, rest = divmod(strip_index, PROJECTIONS * STRIPS)
             i, h = divmod(rest, STRIPS)
             strip = slice(h * P, (h + 1) * P)
@@ -228,9 +234,15 @@ def tile_selfscaleddotproductattention2d_pa_kernel(
                         stop=(g == PASSES - 1),
                     )
                 out_cols = slice(oc * BANK, (oc + 1) * BANK)
-                nc.vector.tensor_tensor(
-                    out=result[:, out_cols], in0=acc[:], in1=bias_sb[:, i, out_cols], op=ALU.add
-                )
+                if helped and (strip_index * HALVES + oc) % SHARE == 0:
+                    nc.scalar.copy(out=result[:, out_cols], in_=acc[:])
+                    nc.gpsimd.tensor_tensor(
+                        out=result[:, out_cols], in0=result[:, out_cols], in1=bias_sb[:, i, out_cols], op=ALU.add
+                    )
+                else:
+                    nc.vector.tensor_tensor(
+                        out=result[:, out_cols], in0=acc[:], in1=bias_sb[:, i, out_cols], op=ALU.add
+                    )
             nc.sync.dma_start(out=outs[i][n, strip, :], in_=result[:])
 
         for n in range(IMAGES):
@@ -255,16 +267,22 @@ def tile_selfscaleddotproductattention2d_pa_kernel(
             else:
                 banks = image_transposes(1)
             weight_quantise(i, oc, w_grouped)
-            project(projected)
+            project(projected, helped=False)
             projected += 1
 
+        x_lns = {}
         for n in range(1, IMAGES):
-            x_ln = image_gain_and_shift(banks)
+            x_lns[n] = image_gain_and_shift(banks)
             if n + 1 < IMAGES:
                 banks = image_transposes(n + 1)
-            image_quantise(n, x_ln)
-            project(projected)
+            if n < FIRST_LATE_IMAGE:
+                image_quantise(n, x_lns[n])
+            project(projected, helped=False)
             projected += 1
 
-        for strip_index in range(projected, IMAGES * PROJECTIONS * STRIPS):
-            project(strip_index)
+        image_strips = PROJECTIONS * STRIPS
+        for strip_index in range(projected, IMAGES * image_strips):
+            n, strips_before_it = divmod(strip_index + LEAD, image_strips)
+            if strips_before_it == 0 and FIRST_LATE_IMAGE <= n < IMAGES:
+                image_quantise(n, x_lns[n])
+            project(strip_index, helped=True)

from contextlib import ExitStack

import concourse.mybir as mybir
from concourse.masks import make_identity

BF16 = mybir.dt.bfloat16
F32 = mybir.dt.float32
U32 = mybir.dt.uint32
U8 = mybir.dt.uint8
FP8X4 = mybir.dt.float8_e4m3fn_x4
ACT = mybir.ActivationFunctionType
ALU = mybir.AluOpType

P = 128
IMAGES = 4
CHANNELS = 1024
IMAGE_PIXELS = 256
OUTPUTS = 1024
PROJECTIONS = 3
EPS = 1e-5

PACK = 4
PASSES = CHANNELS // (P * PACK)
CHUNKS = CHANNELS // P
STRIPS = IMAGE_PIXELS // P
BANK = 512
HALVES = OUTPUTS // BANK
UNIT_BANKS = 4
RUN = 4
SHARE = 3
FIRST_LATE_IMAGE = 2
LEAD = 2
STATS_WIDTH = 512
STATS_CALLS = CHANNELS // STATS_WIDTH
STATS_DIM = 6

FLOPS = 2 * IMAGES * IMAGE_PIXELS * CHANNELS * PROJECTIONS * OUTPUTS


def tile_selfscaleddotproductattention2d_pa_kernel(
    tc, x, ln_gamma, ln_beta, Wq, bq, Wk, bk, Wv, bv, out_0, out_1, out_2
):
    nc = tc.nc
    weights = (Wq, Wk, Wv)
    biases = (bq, bk, bv)
    outs = (out_0, out_1, out_2)

    with ExitStack() as ctx:
        keep = ctx.enter_context(tc.tile_pool(name="keep", bufs=1))
        per_weight = ctx.enter_context(tc.tile_pool(name="per_weight", bufs=PROJECTIONS))
        work = ctx.enter_context(tc.tile_pool(name="work", bufs=2))
        psum_unit = ctx.enter_context(tc.psum_pool(name="psum_unit", bufs=UNIT_BANKS))
        psum_acc = ctx.enter_context(tc.psum_pool(name="psum_acc", bufs=4))
        ctx.enter_context(tc.manual_schedule())

        x_sb = keep.tile([P, IMAGES, CHUNKS // 2, 2 * IMAGE_PIXELS], BF16)
        for n in range(IMAGES):
            nc.sync.dma_start(
                out=x_sb[:, n], in_=x[n].rearrange("(a p e) h w -> p a (e h w)", p=P, e=2)
            )

        gamma_bf = keep.tile([P, CHUNKS], BF16)
        beta_bf = keep.tile([P, CHUNKS], BF16)
        for vector_sb, vector in ((gamma_bf, ln_gamma), (beta_bf, ln_beta)):
            nc.scalar.dma_start(
                out=vector_sb[:].rearrange("p (a e) -> p a e", e=2),
                in_=vector.rearrange("(a p e) -> p a e", p=P, e=2),
            )

        w_sbs = []
        bias_sb = keep.tile([P, PROJECTIONS, OUTPUTS], BF16)
        for i in range(PROJECTIONS):
            w_sb = per_weight.tile([P, OUTPUTS // P, CHANNELS], BF16, name="w_sb")
            rows = weights[i].rearrange("(r p) k -> p r k", p=P)
            for oc in range(HALVES):
                r_range = slice(oc * (BANK // P), (oc + 1) * (BANK // P))
                nc.sync.dma_start(out=w_sb[:, r_range, :], in_=rows[:, r_range, :])
            nc.sync.dma_start(out=bias_sb[:, i, :], in_=biases[i].partition_broadcast(P))
            w_sbs.append(w_sb)

        ident_bf = keep.tile([P, P], BF16)
        make_identity(nc, ident_bf[:])
        ident_f = keep.tile([P, P], F32)
        make_identity(nc, ident_f[:])
        minus_half = keep.tile([P, STRIPS], F32)
        nc.gpsimd.memset(minus_half[:], -0.5)
        gamma = keep.tile([P, CHUNKS], F32)
        beta = keep.tile([P, CHUNKS], F32)
        nc.gpsimd.tensor_copy(out=gamma[:], in_=gamma_bf[:])
        nc.gpsimd.tensor_copy(out=beta[:], in_=beta_bf[:])

        x_pix = keep.tile([P, IMAGES * STRIPS, CHANNELS], BF16)
        mean_var = keep.tile([P, IMAGES * STRIPS, 2], F32)
        var_eps = keep.tile([P, IMAGES * STRIPS], F32)
        rstd = keep.tile([P, IMAGES * STRIPS], F32)
        minus_mean = keep.tile([P, IMAGES * STRIPS], F32)
        x_codes = keep.tile([P, IMAGES, PASSES, IMAGE_PIXELS], U32, align_bytes=64)
        x_scales = keep.tile([P, IMAGES, PASSES, IMAGE_PIXELS], U8, align_bytes=64)
        w_codes = []
        w_scales = []
        for i in range(PROJECTIONS):
            w_codes.append(per_weight.tile([P, HALVES, PASSES, BANK], U32, align_bytes=64, name="w_codes"))
            w_scales.append(per_weight.tile([P, HALVES, PASSES, BANK], U8, align_bytes=64, name="w_scales"))
        normed = []

        def normalise_image(n):
            strips = slice(n * STRIPS, (n + 1) * STRIPS)
            for h in range(STRIPS):
                x_t = psum_unit.tile([P, CHANNELS], BF16, tag="unit", name="x_t")
                for m in range(CHUNKS):
                    a, e = divmod(m, 2)
                    first = e * IMAGE_PIXELS + h * P
                    nc.tensor.transpose(
                        out=x_t[:, m * P : (m + 1) * P],
                        in_=x_sb[:, n, a, first : first + P],
                        identity=ident_bf[:],
                    )
                nc.scalar.copy(out=x_pix[:, n * STRIPS + h, :], in_=x_t[:])
            for h in range(STRIPS):
                b = n * STRIPS + h
                stats = work.tile([P, STATS_CALLS, STATS_DIM], F32)
                for s in range(STATS_CALLS):
                    nc.vector.bn_stats(
                        out=stats[:, s, :], in_=x_pix[:, b, s * STATS_WIDTH : (s + 1) * STATS_WIDTH]
                    )
                nc.vector.bn_aggr(out=mean_var[:, b, :], in_=stats[:].rearrange("p s d -> p (s d)"))
            nc.gpsimd.tensor_scalar(
                out=var_eps[:, strips], in0=mean_var[:, strips, 1], scalar1=EPS, scalar2=1.0,
                op0=ALU.add, op1=ALU.mult,
            )
            nc.gpsimd.tensor_tensor(out=rstd[:, strips], in0=var_eps[:, strips], in1=minus_half[:], op=ALU.pow)
            nc.gpsimd.tensor_scalar(
                out=minus_mean[:, strips], in0=mean_var[:, strips, 0], scalar1=-1.0, scalar2=0.0,
                op0=ALU.mult, op1=ALU.add,
            )
            for h in range(STRIPS):
                b = n * STRIPS + h
                z = keep.tile([P, CHANNELS], F32, name="z%d" % b)
                nc.gpsimd.tensor_scalar(
                    out=z[:], in0=x_pix[:, b, :], scalar1=minus_mean[:, b : b + 1], scalar2=rstd[:, b : b + 1],
                    op0=ALU.add, op1=ALU.mult,
                )
                normed.append(z)

        def image_transposes(n):
            banks = []
            for first_chunk in range(0, CHUNKS, 2):
                z_t = psum_unit.tile([P, 2, IMAGE_PIXELS], F32, tag="unit", name="z_t")
                for c in range(2):
                    m = first_chunk + c
                    for h in range(STRIPS):
                        nc.tensor.transpose(
                            out=z_t[:, c, h * P : (h + 1) * P],
                            in_=normed[n * STRIPS + h][:, m * P : (m + 1) * P],
                            identity=ident_f[:],
                        )
                banks.append(z_t)
            return banks

        def image_gain_and_shift(banks):
            x_ln = work.tile([P, CHUNKS, IMAGE_PIXELS], BF16)
            for m in range(CHUNKS):
                nc.scalar.activation(
                    out=x_ln[:, m, :],
                    in_=banks[m // 2][:, m % 2, :],
                    func=ACT.Identity,
                    bias=beta[:, m : m + 1],
                    scale=gamma[:, m : m + 1],
                )
            return x_ln

        def image_quantise(n, x_ln):
            x_grouped = work.tile([P, PASSES, IMAGE_PIXELS, PACK], BF16, align_bytes=64)
            for g in range(PASSES):
                nc.vector.tensor_copy(
                    out=x_grouped[:, g].rearrange("p (c i) t -> p c t i", i=RUN),
                    in_=x_ln[:, g * PACK : (g + 1) * PACK, :].rearrange("p t (c i) -> p c t i", i=RUN),
                )
            nc.vector.quantize_mx(
                out=x_codes[:, n].rearrange("p g s -> p (g s)").bitcast(FP8X4),
                scales=x_scales[:, n].rearrange("p g s -> p (g s)"),
                in_=x_grouped[:].rearrange("p g s t -> p (g s t)"),
            )

        def weight_transposes(i, oc):
            banks = []
            for g in range(PASSES):
                for pair in range(BANK // (2 * P)):
                    w_t = psum_unit.tile([P, 2, 2 * P], F32, tag="unit", name="w_t")
                    for u in range(2):
                        for rr in range(2):
                            r = oc * (BANK // P) + 2 * pair + rr
                            first = (2 * g + u) * P
                            nc.tensor.transpose(
                                out=w_t[:, u, rr * P : (rr + 1) * P],
                                in_=w_sbs[i][:, r, :].bitcast(F32)[:, first : first + P],
                                identity=ident_f[:],
                            )
                    banks.append(w_t)
            return banks

        def weight_copies(banks):
            w_grouped = work.tile([P, PASSES * BANK * PACK], BF16, align_bytes=64)
            w_grouped_words = w_grouped[:].bitcast(F32)
            for k in range(UNIT_BANKS):
                nc.scalar.copy(
                    out=w_grouped_words[:, k * BANK : (k + 1) * BANK].rearrange("p (o u) -> p o u", u=2),
                    in_=banks[k][:].rearrange("p u o -> p o u"),
                )
            return w_grouped

        def weight_quantise(i, oc, w_grouped):
            nc.vector.quantize_mx(
                out=w_codes[i][:, oc].rearrange("p g o -> p (g o)").bitcast(FP8X4),
                scales=w_scales[i][:, oc].rearrange("p g o -> p (g o)"),
                in_=w_grouped[:],
            )

        def project(strip_index, helped):
            n, rest = divmod(strip_index, PROJECTIONS * STRIPS)
            i, h = divmod(rest, STRIPS)
            strip = slice(h * P, (h + 1) * P)
            result = work.tile([P, OUTPUTS], F32, bufs=4)
            for oc in range(HALVES):
                acc = psum_acc.tile([P, BANK], F32)
                for g in range(PASSES):
                    nc.tensor.matmul_mx(
                        out=acc[:],
                        lhsT=x_codes[:, n, g, strip].bitcast(FP8X4),
                        lhsT_scale=x_scales[:, n, g, strip],
                        rhs=w_codes[i][:, oc, g, :].bitcast(FP8X4),
                        rhs_scale=w_scales[i][:, oc, g, :],
                        start=(g == 0),
                        stop=(g == PASSES - 1),
                    )
                out_cols = slice(oc * BANK, (oc + 1) * BANK)
                if helped and (strip_index * HALVES + oc) % SHARE == 0:
                    nc.scalar.copy(out=result[:, out_cols], in_=acc[:])
                    nc.gpsimd.tensor_tensor(
                        out=result[:, out_cols], in0=result[:, out_cols], in1=bias_sb[:, i, out_cols], op=ALU.add
                    )
                else:
                    nc.vector.tensor_tensor(
                        out=result[:, out_cols], in0=acc[:], in1=bias_sb[:, i, out_cols], op=ALU.add
                    )
            nc.sync.dma_start(out=outs[i][n, strip, :], in_=result[:])

        for n in range(IMAGES):
            normalise_image(n)

        banks = weight_transposes(0, 0)
        w_grouped = weight_copies(banks)
        banks = image_transposes(0)
        weight_quantise(0, 0, w_grouped)

        x_ln = image_gain_and_shift(banks)
        banks = weight_transposes(0, 1)
        image_quantise(0, x_ln)

        projected = 0
        weight_halves = PROJECTIONS * HALVES
        for half_index in range(1, weight_halves):
            i, oc = divmod(half_index, HALVES)
            w_grouped = weight_copies(banks)
            if half_index + 1 < weight_halves:
                banks = weight_transposes((half_index + 1) // HALVES, (half_index + 1) % HALVES)
            else:
                banks = image_transposes(1)
            weight_quantise(i, oc, w_grouped)
            project(projected, helped=False)
            projected += 1

        x_lns = {}
        for n in range(1, IMAGES):
            x_lns[n] = image_gain_and_shift(banks)
            if n + 1 < IMAGES:
                banks = image_transposes(n + 1)
            if n < FIRST_LATE_IMAGE:
                image_quantise(n, x_lns[n])
            project(projected, helped=False)
            projected += 1

        image_strips = PROJECTIONS * STRIPS
        for strip_index in range(projected, IMAGES * image_strips):
            n, strips_before_it = divmod(strip_index + LEAD, image_strips)
            if strips_before_it == 0 and FIRST_LATE_IMAGE <= n < IMAGES:
                image_quantise(n, x_lns[n])
            project(strip_index, helped=True)
